import numpy as np
import ml_dtypes


def mxq(x, axis, fmt="e4m3"):
    dtype, down = {"e4m3": (ml_dtypes.float8_e4m3fn, 7), "e5m2": (ml_dtypes.float8_e5m2, 14)}[fmt]
    v = np.moveaxis(np.asarray(x, np.float32).astype(ml_dtypes.bfloat16).astype(np.float64), axis, -1)
    blocks = v.reshape(v.shape[:-1] + (-1, 32))
    amax = np.abs(blocks).max(-1, keepdims=True)
    byte = np.maximum(np.where(amax > 0, np.frexp(amax)[1] - 1 + 127, 0) - down, 1)
    scale = np.exp2(byte - 127.0)
    codes = (blocks / scale).astype(np.float32).astype(dtype).astype(np.float64)
    return np.moveaxis((codes * scale).reshape(v.shape), -1, axis)


WIDE = False


def mx_kscale(k):
    if not WIDE:
        return np.ones(k)
    levels = np.array([10, -10, 5, -5, 0])
    a = np.random.permutation(np.resize(levels, k // 512 * 4)).reshape(k // 512, 4)
    idx = np.arange(k)
    return np.exp2(a[idx // 512, idx % 128 // 32])


BF16 = ml_dtypes.bfloat16


def bf(x):
    return np.asarray(x, np.float32).astype(BF16)


def f64(x):
    return np.asarray(x).astype(np.float64)


E2M1 = np.array([0.0, 0.5, 1.0, 1.5, 2.0, 3.0, 4.0, 6.0, -0.0, -0.5, -1.0, -1.5, -2.0, -3.0, -4.0, -6.0])


def pack_weight(w, fmt):
    k, n = w.shape
    w = f64(bf(w)).reshape(k // 32, 32, n)
    amax = np.abs(w).max(1)
    if fmt == "e4m3":
        byte = np.frexp(amax)[1] - 1 + 127 - 7
    else:
        mant, ex = np.frexp(amax / 6.0)
        byte = np.where(mant > 0.5, ex, ex - 1) + 127
    byte = np.clip(np.where(amax > 0, byte, 1), 1, 254)
    scaled = (w * np.exp2(127.0 - byte)[:, None, :]).reshape(k, n).astype(np.float32)
    by_word = np.ascontiguousarray(scaled.reshape(k // 512, 128, 4, n).transpose(0, 1, 3, 2))
    if fmt == "e4m3":
        words = by_word.astype(ml_dtypes.float8_e4m3fn).view(np.uint8)
    else:
        c = by_word.astype(ml_dtypes.float4_e2m1fn).view(np.uint8) & 0xF
        words = c[..., 0::2] | (c[..., 1::2] << 4)
    return np.ascontiguousarray(words), np.ascontiguousarray(byte.astype(np.uint8).reshape(k // 512, 16, n))


def unpack_weight(words, scales, fmt):
    g, p, n, _ = words.shape
    if fmt == "e4m3":
        vals = np.ascontiguousarray(words).view(ml_dtypes.float8_e4m3fn).astype(np.float64)
    else:
        nib = np.empty((g, p, n, 4), np.uint8)
        nib[..., 0::2] = words & 0xF
        nib[..., 1::2] = words >> 4
        vals = E2M1[nib]
    vals = vals * np.repeat(np.exp2(scales.astype(np.float64) - 127.0), 8, axis=1)[..., None]
    return vals.transpose(0, 1, 3, 2).reshape(g * 512, n)


N, H, W, K = 512, 2048, 8, 512
TAU = 1.0


def silu(v):
    return v / (1.0 + np.exp(-v))


def softmax_last(v):
    e = np.exp(v - v.max(-1, keepdims=True))
    return e / e.sum(-1, keepdims=True)


def setup_inputs():
    s = np.tile(mx_kscale(K), W)
    x = bf(np.random.standard_normal((N, W * K)) * s)
    t = np.random.standard_normal((H, W * K)) / np.sqrt(K) / s
    words, scales = pack_weight(np.ascontiguousarray(t.T), "e4m3")
    return {"x": x, "template_flat_words": words, "template_flat_scales": scales}


def reference(x, template_flat_words, template_flat_scales):
    n = x.shape[0]
    xw = f64(x).reshape(n, W, K)
    xq = mxq(xw, 2, "e4m3")
    tq = unpack_weight(template_flat_words, template_flat_scales, "e4m3").reshape(W, K, -1)
    s = (xq.transpose(1, 0, 2) @ tq).transpose(1, 2, 0)
    gate = softmax_last(s / TAU)
    return np.sum(gate * silu(s), axis=-1)

@@ -1,0 +1,216 @@
+import concourse.mybir as mybir
+from concourse.masks import make_identity
+
+F32 = mybir.dt.float32
+BF16 = mybir.dt.bfloat16
+I32 = mybir.dt.int32
+U32 = mybir.dt.uint32
+U8 = mybir.dt.uint8
+FP8X4 = mybir.dt.float8_e4m3fn_x4
+ACT = mybir.ActivationFunctionType
+ALU = mybir.AluOpType
+
+P = 128
+ROWS = 512
+FEATURES = 2048
+WINDOWS = 8
+K_WINDOW = 512
+FLOPS = 2 * ROWS * FEATURES * WINDOWS * K_WINDOW
+
+ROW_TILES = ROWS // P
+HALF = 256
+BLOCKS = HALF // P
+HALVES = ROWS // HALF
+FEATURE_TILES = FEATURES // P
+UNITS = FEATURE_TILES * HALVES
+BANKS = 4
+CHUNK_TILES = 4
+CHUNK = CHUNK_TILES * P
+CHUNKS = FEATURES // CHUNK
+GROUP_UNITS = CHUNK_TILES * HALVES
+
+BATCH = 4
+LAG = 5
+
+
+def tile_dendriticlayersilu_ffn_kernel(tc, x, template_flat_words, template_flat_scales, out):
+    nc = tc.nc
+
+    words_dram = (
+        template_flat_words.rearrange("g p h t -> g p (h t)").bitcast(I32).rearrange("g p h -> p g h")
+    )
+    scales_dram = template_flat_scales.bitcast(I32)
+    out_dram = out.rearrange("(b p) h -> p b h", p=P)
+
+    with tc.manual_schedule(), tc.tile_pool(name="keep", bufs=1) as keep, tc.tile_pool(
+        name="weights", bufs=2
+    ) as weights, tc.psum_pool(name="banks", bufs=6) as banks, tc.psum_pool(name="sums", bufs=2) as sums:
+        ident = keep.tile([P, P], F32, name="ident")
+        make_identity(nc, ident[:])
+
+        w_planes = keep.tile([P, WINDOWS // 4, FEATURES], U8, name="w_planes", align_bytes=64)
+        nc.vector.memset(w_planes[:].rearrange("p a h -> p (a h)").bitcast(I32), 0)
+
+        x_codes = keep.tile([P, HALVES, WINDOWS, HALF], U32, name="x_codes", align_bytes=64)
+        x_scales = keep.tile([P, HALVES, WINDOWS, HALF], U8, name="x_scales", align_bytes=64)
+
+        w_chunks = {}
+
+        def load_weights(c):
+            w_chunks[c] = weights.tile([P, WINDOWS, CHUNK], U32, name="w_chunk", align_bytes=64)
+            nc.sync.dma_start(
+                out=w_chunks[c][:].bitcast(I32), in_=words_dram[:, :, c * CHUNK : (c + 1) * CHUNK]
+            )
+
+        with tc.tile_pool(name="rows", bufs=2) as rows, tc.tile_pool(name="grouped", bufs=1) as regroup:
+            for half in range(HALVES):
+                grouped = regroup.tile([P, WINDOWS, HALF, 4], BF16, name="grouped", align_bytes=64)
+                grouped_words = grouped[:].bitcast(F32)
+                for b in range(BLOCKS):
+                    i = half * BLOCKS + b
+                    x_rows = rows.tile([P, WINDOWS * K_WINDOW], BF16, name="x_rows")
+                    nc.sync.dma_start(out=x_rows[:], in_=x[i * P : (i + 1) * P, :])
+                    if i == 1:
+                        for a in range(WINDOWS // 4):
+                            for q in range(4):
+                                nc.sync.dma_start(
+                                    out=w_planes[32 * q : 32 * q + 16, a, :].bitcast(I32),
+                                    in_=scales_dram[4 * a : 4 * a + 4, 4 * q : 4 * q + 4, :],
+                                )
+                        load_weights(0)
+                    x_words = x_rows[:].bitcast(F32)
+                    for pair in range(WINDOWS // 2):
+                        flipped = banks.tile([P, 2, 2, P], F32, name="flipped", tag="bank")
+                        for l in range(2):
+                            g = 2 * pair + l
+                            for u in range(2):
+                                nc.tensor.transpose(
+                                    flipped[:, l, u, :], x_words[:, 256 * g + u : 256 * (g + 1) : 2], ident[:]
+                                )
+                        source = flipped[:].rearrange("p l u n -> p l n u")
+                        target = grouped_words[:, 2 * pair : 2 * pair + 2, b * P : (b + 1) * P, :]
+                        if pair % 2 == 0:
+                            nc.vector.tensor_copy(out=target, in_=source)
+                        else:
+                            nc.scalar.copy(out=target, in_=source)
+                for c in range(2):
+                    four = slice(4 * c, 4 * c + 4)
+                    nc.vector.quantize_mx(
+                        out=x_codes[:, half, four, :].rearrange("p g n -> p (g n)").bitcast(FP8X4),
+                        scales=x_scales[:, half, four, :].rearrange("p g n -> p (g n)"),
+                        in_=grouped[:, four, :, :].rearrange("p g n t -> p (g n t)"),
+                    )
+
+        load_weights(1)
+
+        with tc.tile_pool(name="shifted", bufs=LAG + 2) as shifted_pool, tc.tile_pool(
+            name="gated", bufs=LAG + 2
+        ) as gated_pool, tc.tile_pool(name="small", bufs=2) as small, tc.tile_pool(
+            name="finished", bufs=2
+        ) as finished_pool:
+            score_banks = {}
+            shifted = {}
+            gated = {}
+            finished = {}
+
+            def scores(u):
+                t, half = divmod(u, HALVES)
+                w_chunk = w_chunks[t // CHUNK_TILES]
+                cols = slice((t % CHUNK_TILES) * P, (t % CHUNK_TILES + 1) * P)
+                score_banks[u] = []
+                for j in range(BANKS):
+                    bank = banks.tile([P, 2, HALF], F32, name="score_bank", tag="bank")
+                    score_banks[u].append(bank)
+                    for l in range(2):
+                        g = 2 * j + l
+                        nc.tensor.matmul_mx(
+                            out=bank[:, l, :],
+                            lhsT=w_chunk[:, g, cols].bitcast(FP8X4),
+                            lhsT_scale=w_planes[4 * (g % 4) : P, g // 4, t * P : (t + 1) * P],
+                            rhs=x_codes[:, half, g, :].bitcast(FP8X4),
+                            rhs_scale=x_scales[:, half, g, :],
+                            start=True,
+                            stop=True,
+                        )
+
+            def silu(u):
+                gated[u] = gated_pool.tile([P, WINDOWS, HALF], F32, name="gated")
+                for j in range(BANKS):
+                    nc.scalar.activation(
+                        out=gated[u][:, 2 * j : 2 * j + 2, :], in_=score_banks[u][j][:], func=ACT.Silu
+                    )
+
+            def shift(u):
+                lane_max = small.tile([P, 2, HALF], F32, name="lane_max")
+                nc.vector.tensor_copy(out=lane_max[:], in_=score_banks[u][0][:])
+                for j in range(1, BANKS):
+                    nc.vector.tensor_tensor(
+                        out=lane_max[:], in0=score_banks[u][j][:], in1=lane_max[:], op=ALU.max
+                    )
+                top = small.tile([P, HALF], F32, name="top")
+                nc.vector.tensor_tensor(out=top[:], in0=lane_max[:, 0, :], in1=lane_max[:, 1, :], op=ALU.max)
+                shifted[u] = shifted_pool.tile([P, WINDOWS, HALF], F32, name="shifted")
+                for j in range(BANKS):
+                    nc.vector.tensor_tensor(
+                        out=shifted[u][:, 2 * j : 2 * j + 2, :],
+                        in0=score_banks[u][j][:],
+                        in1=top[:].unsqueeze(1).to_broadcast([P, 2, HALF]),
+                        op=ALU.subtract,
+                    )
+
+            def weigh(u):
+                nc.scalar.activation(out=shifted[u][:], in_=shifted[u][:], func=ACT.Exp)
+                multiplier = nc.gpsimd if u < UNITS - BATCH else nc.vector
+                multiplier.tensor_tensor(out=gated[u][:], in0=shifted[u][:], in1=gated[u][:], op=ALU.mult)
+
+            def window_sums(u):
+                t, half = divmod(u, HALVES)
+                group = t // CHUNK_TILES
+                if u % GROUP_UNITS == 0:
+                    finished[group] = finished_pool.tile([P, 2, ROW_TILES, CHUNK], F32, name="finished")
+                both = sums.tile([P, 2, BLOCKS, P], F32, name="both")
+                for which, terms in enumerate((shifted[u], gated[u])):
+                    for b in range(BLOCKS):
+                        for w in range(WINDOWS):
+                            nc.tensor.matmul(
+                                out=both[:, which, b, :],
+                                lhsT=terms[:, w, b * P : (b + 1) * P],
+                                rhs=ident[:],
+                                is_transpose=True,
+                                start=(w == 0),
+                                stop=(w == WINDOWS - 1),
+                            )
+                nc.vector.tensor_copy(
+                    out=finished[group][
+                        :, :, half * BLOCKS : (half + 1) * BLOCKS, (t % CHUNK_TILES) * P : (t % CHUNK_TILES + 1) * P
+                    ],
+                    in_=both[:],
+                )
+
+            def divide_and_store(group):
+                denominator = finished[group][:, 0, :, :]
+                numerator = finished[group][:, 1, :, :]
+                nc.scalar.activation(out=denominator, in_=denominator, func=ACT.Ln)
+                nc.scalar.activation(out=denominator, in_=denominator, func=ACT.Exp, scale=-1.0)
+                nc.gpsimd.tensor_tensor(out=numerator, in0=numerator, in1=denominator, op=ALU.mult)
+                nc.sync.dma_start(out=out_dram[:, :, group * CHUNK : (group + 1) * CHUNK], in_=numerator)
+
+            stored = 0
+            for step in range(UNITS + LAG):
+                if step < UNITS:
+                    if step % GROUP_UNITS == 0 and 0 < step // GROUP_UNITS < CHUNKS - 1:
+                        load_weights(step // GROUP_UNITS + 1)
+                    scores(step)
+                    silu(step)
+                    shift(step)
+                if step >= LAG:
+                    window_sums(step - LAG)
+                if step % BATCH == BATCH - 1 and step < UNITS:
+                    if (stored + 1) * GROUP_UNITS + LAG + 2 <= step + 1:
+                        divide_and_store(stored)
+                        stored += 1
+                    for u in range(step - BATCH + 1, step + 1):
+                        weigh(u)
+            while stored < CHUNKS:
+                divide_and_store(stored)
+                stored += 1

@@ -27,10 +27,10 @@ BANKS = 4
 CHUNK_TILES = 4
 CHUNK = CHUNK_TILES * P
 CHUNKS = FEATURES // CHUNK
-GROUP_UNITS = CHUNK_TILES * HALVES
+CHUNK_UNITS = CHUNK_TILES * HALVES
 
-BATCH = 4
-LAG = 5
+SUM_LAG = 2
+KEEP_LAG = 3
 
 
 def tile_dendriticlayersilu_ffn_kernel(tc, x, template_flat_words, template_flat_scales, out):
@@ -53,6 +53,8 @@ def tile_dendriticlayersilu_ffn_kernel(tc, x, template_flat_words, template_flat
 
         x_codes = keep.tile([P, HALVES, WINDOWS, HALF], U32, name="x_codes", align_bytes=64)
         x_scales = keep.tile([P, HALVES, WINDOWS, HALF], U8, name="x_scales", align_bytes=64)
+
+        totals = keep.tile([P, 2, ROW_TILES, FEATURES], F32, name="totals")
 
         w_chunks = {}
 
@@ -103,24 +105,23 @@ def tile_dendriticlayersilu_ffn_kernel(tc, x, template_flat_words, template_flat
 
         load_weights(1)
 
-        with tc.tile_pool(name="shifted", bufs=LAG + 2) as shifted_pool, tc.tile_pool(
-            name="gated", bufs=LAG + 2
-        ) as gated_pool, tc.tile_pool(name="small", bufs=2) as small, tc.tile_pool(
-            name="finished", bufs=2
-        ) as finished_pool:
+        with tc.tile_pool(name="shifted", bufs=4) as shifted_pool, tc.tile_pool(
+            name="gated", bufs=4
+        ) as gated_pool, tc.tile_pool(name="small", bufs=2) as small:
             score_banks = {}
+            first_bank = {}
+            top = {}
             shifted = {}
             gated = {}
-            finished = {}
+            both_sums = {}
 
-            def scores(u):
+            def scores(u, which_banks):
                 t, half = divmod(u, HALVES)
                 w_chunk = w_chunks[t // CHUNK_TILES]
                 cols = slice((t % CHUNK_TILES) * P, (t % CHUNK_TILES + 1) * P)
-                score_banks[u] = []
-                for j in range(BANKS):
+                for j in which_banks:
                     bank = banks.tile([P, 2, HALF], F32, name="score_bank", tag="bank")
-                    score_banks[u].append(bank)
+                    score_banks[u, j] = bank
                     for l in range(2):
                         g = 2 * j + l
                         nc.tensor.matmul_mx(
@@ -133,84 +134,107 @@ def tile_dendriticlayersilu_ffn_kernel(tc, x, template_flat_words, template_flat
                             stop=True,
                         )
 
-            def silu(u):
-                gated[u] = gated_pool.tile([P, WINDOWS, HALF], F32, name="gated")
-                for j in range(BANKS):
+            def half_tanh(u, which_banks):
+                for j in which_banks:
+                    if j == 0:
+                        gated[u] = gated_pool.tile([P, WINDOWS, HALF], F32, name="gated")
+                        first_bank[u] = small.tile([P, 2, HALF], F32, name="first_bank")
+                        nc.scalar.copy(out=first_bank[u][:], in_=score_banks[u, 0][:])
                     nc.scalar.activation(
-                        out=gated[u][:, 2 * j : 2 * j + 2, :], in_=score_banks[u][j][:], func=ACT.Silu
+                        out=gated[u][:, 2 * j : 2 * j + 2, :], in_=score_banks[u, j][:], func=ACT.Tanh, scale=0.5
                     )
 
             def shift(u):
                 lane_max = small.tile([P, 2, HALF], F32, name="lane_max")
-                nc.vector.tensor_copy(out=lane_max[:], in_=score_banks[u][0][:])
+                nc.vector.tensor_tensor(
+                    out=lane_max[:], in0=score_banks[u, 1][:], in1=first_bank[u][:], op=ALU.max
+                )
+                for j in range(2, BANKS):
+                    nc.vector.tensor_tensor(
+                        out=lane_max[:], in0=score_banks[u, j][:], in1=lane_max[:], op=ALU.max
+                    )
+                top[u] = small.tile([P, HALF], F32, name="top")
+                nc.vector.tensor_tensor(
+                    out=top[u][:], in0=lane_max[:, 0, :], in1=lane_max[:, 1, :], op=ALU.max
+                )
+                top_twice = top[u][:].unsqueeze(1).to_broadcast([P, 2, HALF])
+                shifted[u] = shifted_pool.tile([P, WINDOWS, HALF], F32, name="shifted")
+                nc.gpsimd.tensor_tensor(
+                    out=shifted[u][:, 0:2, :], in0=first_bank[u][:], in1=top_twice, op=ALU.subtract
+                )
                 for j in range(1, BANKS):
                     nc.vector.tensor_tensor(
-                        out=lane_max[:], in0=score_banks[u][j][:], in1=lane_max[:], op=ALU.max
-                    )
-                top = small.tile([P, HALF], F32, name="top")
-                nc.vector.tensor_tensor(out=top[:], in0=lane_max[:, 0, :], in1=lane_max[:, 1, :], op=ALU.max)
-                shifted[u] = shifted_pool.tile([P, WINDOWS, HALF], F32, name="shifted")
-                for j in range(BANKS):
-                    nc.vector.tensor_tensor(
                         out=shifted[u][:, 2 * j : 2 * j + 2, :],
-                        in0=score_banks[u][j][:],
-                        in1=top[:].unsqueeze(1).to_broadcast([P, 2, HALF]),
+                        in0=score_banks[u, j][:],
+                        in1=top_twice,
                         op=ALU.subtract,
+                    )
+
+            def gate(u):
+                for j in range(BANKS):
+                    z = gated[u][:, 2 * j : 2 * j + 2, :]
+                    nc.vector.scalar_tensor_tensor(
+                        out=z, in0=z, scalar=1.0, in1=score_banks[u, j][:], op0=ALU.add, op1=ALU.mult
                     )
 
             def weigh(u):
                 nc.scalar.activation(out=shifted[u][:], in_=shifted[u][:], func=ACT.Exp)
-                multiplier = nc.gpsimd if u < UNITS - BATCH else nc.vector
-                multiplier.tensor_tensor(out=gated[u][:], in0=shifted[u][:], in1=gated[u][:], op=ALU.mult)
+                nc.gpsimd.tensor_tensor(out=gated[u][:], in0=shifted[u][:], in1=gated[u][:], op=ALU.mult)
 
             def window_sums(u):
-                t, half = divmod(u, HALVES)
-                group = t // CHUNK_TILES
-                if u % GROUP_UNITS == 0:
-                    finished[group] = finished_pool.tile([P, 2, ROW_TILES, CHUNK], F32, name="finished")
-                both = sums.tile([P, 2, BLOCKS, P], F32, name="both")
+                both_sums[u] = sums.tile([P, 2, BLOCKS, P], F32, name="both_sums")
                 for which, terms in enumerate((shifted[u], gated[u])):
                     for b in range(BLOCKS):
                         for w in range(WINDOWS):
                             nc.tensor.matmul(
-                                out=both[:, which, b, :],
+                                out=both_sums[u][:, which, b, :],
                                 lhsT=terms[:, w, b * P : (b + 1) * P],
                                 rhs=ident[:],
                                 is_transpose=True,
                                 start=(w == 0),
                                 stop=(w == WINDOWS - 1),
                             )
-                nc.vector.tensor_copy(
-                    out=finished[group][
-                        :, :, half * BLOCKS : (half + 1) * BLOCKS, (t % CHUNK_TILES) * P : (t % CHUNK_TILES + 1) * P
-                    ],
-                    in_=both[:],
+
+            def keep_sums(u):
+                t, half = divmod(u, HALVES)
+                nc.scalar.copy(
+                    out=totals[:, :, half * BLOCKS : (half + 1) * BLOCKS, t * P : (t + 1) * P],
+                    in_=both_sums[u][:],
                 )
 
-            def divide_and_store(group):
-                denominator = finished[group][:, 0, :, :]
-                numerator = finished[group][:, 1, :, :]
-                nc.scalar.activation(out=denominator, in_=denominator, func=ACT.Ln)
-                nc.scalar.activation(out=denominator, in_=denominator, func=ACT.Exp, scale=-1.0)
-                nc.gpsimd.tensor_tensor(out=numerator, in0=numerator, in1=denominator, op=ALU.mult)
-                nc.sync.dma_start(out=out_dram[:, :, group * CHUNK : (group + 1) * CHUNK], in_=numerator)
+            early, late = (0, 1), (2, 3)
+            scores(0, early + late)
+            half_tanh(0, early + late)
+            for u in range(UNITS + KEEP_LAG):
+                following = u + 1
+                if following < UNITS:
+                    if following % CHUNK_UNITS == 0 and following // CHUNK_UNITS + 1 < CHUNKS:
+                        load_weights(following // CHUNK_UNITS + 1)
+                    scores(following, early)
+                if 0 <= u - SUM_LAG < UNITS:
+                    window_sums(u - SUM_LAG)
+                if u < UNITS:
+                    shift(u)
+                if 0 <= u - 1 < UNITS:
+                    weigh(u - 1)
+                if u >= KEEP_LAG:
+                    keep_sums(u - KEEP_LAG)
+                if following < UNITS:
+                    half_tanh(following, early)
+                if u < UNITS:
+                    gate(u)
+                if following < UNITS:
+                    scores(following, late)
+                    half_tanh(following, late)
 
-            stored = 0
-            for step in range(UNITS + LAG):
-                if step < UNITS:
-                    if step % GROUP_UNITS == 0 and 0 < step // GROUP_UNITS < CHUNKS - 1:
-                        load_weights(step // GROUP_UNITS + 1)
-                    scores(step)
-                    silu(step)
-                    shift(step)
-                if step >= LAG:
-                    window_sums(step - LAG)
-                if step % BATCH == BATCH - 1 and step < UNITS:
-                    if (stored + 1) * GROUP_UNITS + LAG + 2 <= step + 1:
-                        divide_and_store(stored)
-                        stored += 1
-                    for u in range(step - BATCH + 1, step + 1):
-                        weigh(u)
-            while stored < CHUNKS:
-                divide_and_store(stored)
-                stored += 1
+            for c in range(CHUNKS):
+                denominator = totals[:, 0, :, c * CHUNK : (c + 1) * CHUNK]
+                nc.scalar.activation(out=denominator, in_=denominator, func=ACT.Ln)
+            for c in range(CHUNKS):
+                denominator = totals[:, 0, :, c * CHUNK : (c + 1) * CHUNK]
+                numerator = totals[:, 1, :, c * CHUNK : (c + 1) * CHUNK]
+                nc.scalar.activation(out=denominator, in_=denominator, func=ACT.Exp, scale=-1.0)
+                nc.vector.scalar_tensor_tensor(
+                    out=numerator, in0=numerator, scalar=0.5, in1=denominator, op0=ALU.mult, op1=ALU.mult
+                )
+                nc.sync.dma_start(out=out_dram[:, :, c * CHUNK : (c + 1) * CHUNK], in_=numerator)

@@ -29,8 +29,8 @@ CHUNK = CHUNK_TILES * P
 CHUNKS = FEATURES // CHUNK
 CHUNK_UNITS = CHUNK_TILES * HALVES
 
-SUM_LAG = 2
-KEEP_LAG = 3
+SUM_LAG = 3
+KEEP_LAG = 4
 
 
 def tile_dendriticlayersilu_ffn_kernel(tc, x, template_flat_words, template_flat_scales, out):
@@ -105,8 +105,8 @@ def tile_dendriticlayersilu_ffn_kernel(tc, x, template_flat_words, template_flat
 
         load_weights(1)
 
-        with tc.tile_pool(name="shifted", bufs=4) as shifted_pool, tc.tile_pool(
-            name="gated", bufs=4
+        with tc.tile_pool(name="shifted", bufs=5) as shifted_pool, tc.tile_pool(
+            name="gated", bufs=5
         ) as gated_pool, tc.tile_pool(name="small", bufs=2) as small:
             score_banks = {}
             first_bank = {}
@@ -144,19 +144,28 @@ def tile_dendriticlayersilu_ffn_kernel(tc, x, template_flat_words, template_flat
                         out=gated[u][:, 2 * j : 2 * j + 2, :], in_=score_banks[u, j][:], func=ACT.Tanh, scale=0.5
                     )
 
-            def shift(u):
+            def shift_and_gate(u):
+                def gate(j):
+                    z = gated[u][:, 2 * j : 2 * j + 2, :]
+                    nc.vector.scalar_tensor_tensor(
+                        out=z, in0=z, scalar=1.0, in1=score_banks[u, j][:], op0=ALU.add, op1=ALU.mult
+                    )
+
                 lane_max = small.tile([P, 2, HALF], F32, name="lane_max")
                 nc.vector.tensor_tensor(
                     out=lane_max[:], in0=score_banks[u, 1][:], in1=first_bank[u][:], op=ALU.max
                 )
+                gate(0)
                 for j in range(2, BANKS):
                     nc.vector.tensor_tensor(
                         out=lane_max[:], in0=score_banks[u, j][:], in1=lane_max[:], op=ALU.max
                     )
+                    gate(j - 1)
                 top[u] = small.tile([P, HALF], F32, name="top")
                 nc.vector.tensor_tensor(
                     out=top[u][:], in0=lane_max[:, 0, :], in1=lane_max[:, 1, :], op=ALU.max
                 )
+                gate(BANKS - 1)
                 top_twice = top[u][:].unsqueeze(1).to_broadcast([P, 2, HALF])
                 shifted[u] = shifted_pool.tile([P, WINDOWS, HALF], F32, name="shifted")
                 nc.gpsimd.tensor_tensor(
@@ -168,13 +177,6 @@ def tile_dendriticlayersilu_ffn_kernel(tc, x, template_flat_words, template_flat
                         in0=score_banks[u, j][:],
                         in1=top_twice,
                         op=ALU.subtract,
-                    )
-
-            def gate(u):
-                for j in range(BANKS):
-                    z = gated[u][:, 2 * j : 2 * j + 2, :]
-                    nc.vector.scalar_tensor_tensor(
-                        out=z, in0=z, scalar=1.0, in1=score_banks[u, j][:], op0=ALU.add, op1=ALU.mult
                     )
 
             def weigh(u):
@@ -214,15 +216,13 @@ def tile_dendriticlayersilu_ffn_kernel(tc, x, template_flat_words, template_flat
                 if 0 <= u - SUM_LAG < UNITS:
                     window_sums(u - SUM_LAG)
                 if u < UNITS:
-                    shift(u)
+                    shift_and_gate(u)
                 if 0 <= u - 1 < UNITS:
                     weigh(u - 1)
                 if u >= KEEP_LAG:
                     keep_sums(u - KEEP_LAG)
                 if following < UNITS:
                     half_tanh(following, early)
-                if u < UNITS:
-                    gate(u)
                 if following < UNITS:
                     scores(following, late)
                     half_tanh(following, late)

@@ -9,6 +9,7 @@ U8 = mybir.dt.uint8
 FP8X4 = mybir.dt.float8_e4m3fn_x4
 ACT = mybir.ActivationFunctionType
 ALU = mybir.AluOpType
+AXIS = mybir.AxisListType
 
 P = 128
 ROWS = 512
@@ -162,8 +163,8 @@ def tile_dendriticlayersilu_ffn_kernel(tc, x, template_flat_words, template_flat
                     )
                     gate(j - 1)
                 top[u] = small.tile([P, HALF], F32, name="top")
-                nc.vector.tensor_tensor(
-                    out=top[u][:], in0=lane_max[:, 0, :], in1=lane_max[:, 1, :], op=ALU.max
+                nc.vector.tensor_reduce(
+                    out=top[u][:], in_=lane_max[:].rearrange("p l n -> p n l"), op=ALU.max, axis=AXIS.X
                 )
                 gate(BANKS - 1)
                 top_twice = top[u][:].unsqueeze(1).to_broadcast([P, 2, HALF])

@@ -25,13 +25,20 @@ HALVES = ROWS // HALF
 FEATURE_TILES = FEATURES // P
 UNITS = FEATURE_TILES * HALVES
 BANKS = 4
+PAIRS = WINDOWS // 2
 CHUNK_TILES = 4
 CHUNK = CHUNK_TILES * P
 CHUNKS = FEATURES // CHUNK
 CHUNK_UNITS = CHUNK_TILES * HALVES
 
-SUM_LAG = 3
-KEEP_LAG = 4
+DENOMINATOR_LAG = 2
+NUMERATOR_LAG = 3
+
+
+def place(u):
+    c, rest = divmod(u, CHUNK_UNITS)
+    half, i = divmod(rest, CHUNK_TILES)
+    return c, half, c * CHUNK_TILES + i
 
 
 def tile_dendriticlayersilu_ffn_kernel(tc, x, template_flat_words, template_flat_scales, out):
@@ -45,12 +52,22 @@ def tile_dendriticlayersilu_ffn_kernel(tc, x, template_flat_words, template_flat
 
     with tc.manual_schedule(), tc.tile_pool(name="keep", bufs=1) as keep, tc.tile_pool(
         name="weights", bufs=2
-    ) as weights, tc.psum_pool(name="banks", bufs=6) as banks, tc.psum_pool(name="sums", bufs=2) as sums:
+    ) as weights, tc.tile_pool(name="rows", bufs=2 * PAIRS) as rows, tc.tile_pool(
+        name="grouped", bufs=3
+    ) as regroup, tc.tile_pool(name="shifted", bufs=4) as shifted_pool, tc.tile_pool(
+        name="gated", bufs=5
+    ) as gated_pool, tc.tile_pool(name="small", bufs=2) as small, tc.psum_pool(
+        name="banks", bufs=6
+    ) as banks, tc.psum_pool(name="sums", bufs=2) as sums:
+        w_planes = keep.tile([P, WINDOWS // 4, FEATURES], U8, name="w_planes", align_bytes=64)
+        nc.vector.memset(w_planes[:].rearrange("p a h -> p (a h)").bitcast(I32), 0)
+
         ident = keep.tile([P, P], F32, name="ident")
         make_identity(nc, ident[:])
 
-        w_planes = keep.tile([P, WINDOWS // 4, FEATURES], U8, name="w_planes", align_bytes=64)
-        nc.vector.memset(w_planes[:].rearrange("p a h -> p (a h)").bitcast(I32), 0)
+        warm = keep.tile([P, 2], F32, name="warm")
+        nc.vector.memset(warm[:], 0.0)
+        nc.scalar.activation(out=warm[:, 1:2], in_=warm[:, 0:1], func=ACT.Tanh)
 
         x_codes = keep.tile([P, HALVES, WINDOWS, HALF], U32, name="x_codes", align_bytes=64)
         x_scales = keep.tile([P, HALVES, WINDOWS, HALF], U8, name="x_scales", align_bytes=64)
@@ -59,183 +76,240 @@ def tile_dendriticlayersilu_ffn_kernel(tc, x, template_flat_words, template_flat
 
         w_chunks = {}
 
-        def load_weights(c):
-            w_chunks[c] = weights.tile([P, WINDOWS, CHUNK], U32, name="w_chunk", align_bytes=64)
+        def load_weights(c, tiles):
+            if c not in w_chunks:
+                w_chunks[c] = weights.tile([P, WINDOWS, CHUNK], U32, name="w_chunk", align_bytes=64)
+            cols = slice(tiles[0] * P, (tiles[-1] + 1) * P)
             nc.sync.dma_start(
-                out=w_chunks[c][:].bitcast(I32), in_=words_dram[:, :, c * CHUNK : (c + 1) * CHUNK]
+                out=w_chunks[c][:, :, cols].bitcast(I32),
+                in_=words_dram[:, :, c * CHUNK + cols.start : c * CHUNK + cols.stop],
             )
 
-        with tc.tile_pool(name="rows", bufs=2) as rows, tc.tile_pool(name="grouped", bufs=1) as regroup:
-            for half in range(HALVES):
-                grouped = regroup.tile([P, WINDOWS, HALF, 4], BF16, name="grouped", align_bytes=64)
-                grouped_words = grouped[:].bitcast(F32)
-                for b in range(BLOCKS):
-                    i = half * BLOCKS + b
-                    x_rows = rows.tile([P, WINDOWS * K_WINDOW], BF16, name="x_rows")
-                    nc.sync.dma_start(out=x_rows[:], in_=x[i * P : (i + 1) * P, :])
-                    if i == 1:
-                        for a in range(WINDOWS // 4):
-                            for q in range(4):
-                                nc.sync.dma_start(
-                                    out=w_planes[32 * q : 32 * q + 16, a, :].bitcast(I32),
-                                    in_=scales_dram[4 * a : 4 * a + 4, 4 * q : 4 * q + 4, :],
-                                )
-                        load_weights(0)
-                    x_words = x_rows[:].bitcast(F32)
-                    for pair in range(WINDOWS // 2):
-                        flipped = banks.tile([P, 2, 2, P], F32, name="flipped", tag="bank")
-                        for l in range(2):
-                            g = 2 * pair + l
-                            for u in range(2):
-                                nc.tensor.transpose(
-                                    flipped[:, l, u, :], x_words[:, 256 * g + u : 256 * (g + 1) : 2], ident[:]
-                                )
-                        source = flipped[:].rearrange("p l u n -> p l n u")
-                        target = grouped_words[:, 2 * pair : 2 * pair + 2, b * P : (b + 1) * P, :]
-                        if pair % 2 == 0:
-                            nc.vector.tensor_copy(out=target, in_=source)
-                        else:
-                            nc.scalar.copy(out=target, in_=source)
-                for c in range(2):
-                    four = slice(4 * c, 4 * c + 4)
-                    nc.vector.quantize_mx(
-                        out=x_codes[:, half, four, :].rearrange("p g n -> p (g n)").bitcast(FP8X4),
-                        scales=x_scales[:, half, four, :].rearrange("p g n -> p (g n)"),
-                        in_=grouped[:, four, :, :].rearrange("p g n t -> p (g n t)"),
+        def load_planes():
+            for a in range(WINDOWS // 4):
+                for q in range(4):
+                    nc.sync.dma_start(
+                        out=w_planes[32 * q : 32 * q + 16, a, :].bitcast(I32),
+                        in_=scales_dram[4 * a : 4 * a + 4, 4 * q : 4 * q + 4, :],
                     )
 
-        load_weights(1)
+        x_rows = {}
+        flipped = {}
+        grouped = {}
 
-        with tc.tile_pool(name="shifted", bufs=5) as shifted_pool, tc.tile_pool(
-            name="gated", bufs=5
-        ) as gated_pool, tc.tile_pool(name="small", bufs=2) as small:
-            score_banks = {}
-            first_bank = {}
-            top = {}
-            shifted = {}
-            gated = {}
-            both_sums = {}
+        def load_rows(half, pair):
+            for b in range(BLOCKS):
+                i = half * BLOCKS + b
+                x_rows[half, pair, b] = rows.tile([P, 2 * K_WINDOW], BF16, name="x_rows")
+                nc.sync.dma_start(
+                    out=x_rows[half, pair, b][:],
+                    in_=x[i * P : (i + 1) * P, 2 * pair * K_WINDOW : 2 * (pair + 1) * K_WINDOW],
+                )
 
-            def scores(u, which_banks):
-                t, half = divmod(u, HALVES)
-                w_chunk = w_chunks[t // CHUNK_TILES]
-                cols = slice((t % CHUNK_TILES) * P, (t % CHUNK_TILES + 1) * P)
-                for j in which_banks:
-                    bank = banks.tile([P, 2, HALF], F32, name="score_bank", tag="bank")
-                    score_banks[u, j] = bank
-                    for l in range(2):
-                        g = 2 * j + l
-                        nc.tensor.matmul_mx(
-                            out=bank[:, l, :],
-                            lhsT=w_chunk[:, g, cols].bitcast(FP8X4),
-                            lhsT_scale=w_planes[4 * (g % 4) : P, g // 4, t * P : (t + 1) * P],
-                            rhs=x_codes[:, half, g, :].bitcast(FP8X4),
-                            rhs_scale=x_scales[:, half, g, :],
-                            start=True,
-                            stop=True,
+        def flip(half, pair, pool, tag):
+            for b in range(BLOCKS):
+                flipped[half, pair, b] = pool.tile([P, 2, 2, P], F32, name="flipped", tag=tag)
+                x_words = x_rows[half, pair, b][:].bitcast(F32)
+                for l in range(2):
+                    for w in range(2):
+                        nc.tensor.transpose(
+                            flipped[half, pair, b][:, l, w, :], x_words[:, 256 * l + w : 256 * (l + 1) : 2], ident[:]
                         )
 
-            def half_tanh(u, which_banks):
-                for j in which_banks:
-                    if j == 0:
-                        gated[u] = gated_pool.tile([P, WINDOWS, HALF], F32, name="gated")
-                        first_bank[u] = small.tile([P, 2, HALF], F32, name="first_bank")
-                        nc.scalar.copy(out=first_bank[u][:], in_=score_banks[u, 0][:])
-                    nc.scalar.activation(
-                        out=gated[u][:, 2 * j : 2 * j + 2, :], in_=score_banks[u, j][:], func=ACT.Tanh, scale=0.5
+        def regroup_block(half, pair, b, copy):
+            if b == 0:
+                grouped[half, pair] = regroup.tile([P, 2, HALF, 4], BF16, name="grouped", align_bytes=64)
+            copy(
+                out=grouped[half, pair][:].bitcast(F32)[:, :, b * P : (b + 1) * P, :],
+                in_=flipped[half, pair, b][:].rearrange("p l w n -> p l n w"),
+            )
+
+        def quantise(half, pair):
+            two = slice(2 * pair, 2 * pair + 2)
+            nc.vector.quantize_mx(
+                out=x_codes[:, half, two, :].rearrange("p g n -> p (g n)").bitcast(FP8X4),
+                scales=x_scales[:, half, two, :].rearrange("p g n -> p (g n)"),
+                in_=grouped[half, pair][:].rearrange("p g n t -> p (g n t)"),
+            )
+
+        score_banks = {}
+        first_bank = {}
+        top = {}
+        shifted = {}
+        gated = {}
+        both_sums = {}
+
+        def scores(u, which_banks):
+            c, half, t = place(u)
+            cols = slice((t % CHUNK_TILES) * P, (t % CHUNK_TILES + 1) * P)
+            for j in which_banks:
+                bank = banks.tile([P, 2, HALF], F32, name="score_bank", tag="bank")
+                score_banks[u, j] = bank
+                for l in range(2):
+                    g = 2 * j + l
+                    nc.tensor.matmul_mx(
+                        out=bank[:, l, :],
+                        lhsT=w_chunks[c][:, g, cols].bitcast(FP8X4),
+                        lhsT_scale=w_planes[4 * (g % 4) : P, g // 4, t * P : (t + 1) * P],
+                        rhs=x_codes[:, half, g, :].bitcast(FP8X4),
+                        rhs_scale=x_scales[:, half, g, :],
+                        start=True,
+                        stop=True,
                     )
 
-            def shift_and_gate(u):
-                def gate(j):
-                    z = gated[u][:, 2 * j : 2 * j + 2, :]
-                    nc.vector.scalar_tensor_tensor(
-                        out=z, in0=z, scalar=1.0, in1=score_banks[u, j][:], op0=ALU.add, op1=ALU.mult
-                    )
-
-                lane_max = small.tile([P, 2, HALF], F32, name="lane_max")
-                nc.vector.tensor_tensor(
-                    out=lane_max[:], in0=score_banks[u, 1][:], in1=first_bank[u][:], op=ALU.max
-                )
-                gate(0)
-                for j in range(2, BANKS):
-                    nc.vector.tensor_tensor(
-                        out=lane_max[:], in0=score_banks[u, j][:], in1=lane_max[:], op=ALU.max
-                    )
-                    gate(j - 1)
-                top[u] = small.tile([P, HALF], F32, name="top")
-                nc.vector.tensor_reduce(
-                    out=top[u][:], in_=lane_max[:].rearrange("p l n -> p n l"), op=ALU.max, axis=AXIS.X
-                )
-                gate(BANKS - 1)
-                top_twice = top[u][:].unsqueeze(1).to_broadcast([P, 2, HALF])
-                shifted[u] = shifted_pool.tile([P, WINDOWS, HALF], F32, name="shifted")
-                nc.gpsimd.tensor_tensor(
-                    out=shifted[u][:, 0:2, :], in0=first_bank[u][:], in1=top_twice, op=ALU.subtract
-                )
-                for j in range(1, BANKS):
-                    nc.vector.tensor_tensor(
-                        out=shifted[u][:, 2 * j : 2 * j + 2, :],
-                        in0=score_banks[u, j][:],
-                        in1=top_twice,
-                        op=ALU.subtract,
-                    )
-
-            def weigh(u):
-                nc.scalar.activation(out=shifted[u][:], in_=shifted[u][:], func=ACT.Exp)
-                nc.gpsimd.tensor_tensor(out=gated[u][:], in0=shifted[u][:], in1=gated[u][:], op=ALU.mult)
-
-            def window_sums(u):
-                both_sums[u] = sums.tile([P, 2, BLOCKS, P], F32, name="both_sums")
-                for which, terms in enumerate((shifted[u], gated[u])):
-                    for b in range(BLOCKS):
-                        for w in range(WINDOWS):
-                            nc.tensor.matmul(
-                                out=both_sums[u][:, which, b, :],
-                                lhsT=terms[:, w, b * P : (b + 1) * P],
-                                rhs=ident[:],
-                                is_transpose=True,
-                                start=(w == 0),
-                                stop=(w == WINDOWS - 1),
-                            )
-
-            def keep_sums(u):
-                t, half = divmod(u, HALVES)
-                nc.scalar.copy(
-                    out=totals[:, :, half * BLOCKS : (half + 1) * BLOCKS, t * P : (t + 1) * P],
-                    in_=both_sums[u][:],
+        def half_tanh(u, which_banks):
+            for j in which_banks:
+                if j == 0:
+                    gated[u] = gated_pool.tile([P, WINDOWS, HALF], F32, name="gated")
+                    first_bank[u] = small.tile([P, 2, HALF], F32, name="first_bank")
+                    nc.scalar.copy(out=first_bank[u][:], in_=score_banks[u, 0][:])
+                nc.scalar.activation(
+                    out=gated[u][:, 2 * j : 2 * j + 2, :], in_=score_banks[u, j][:], func=ACT.Tanh, scale=0.5
                 )
 
-            early, late = (0, 1), (2, 3)
-            scores(0, early + late)
-            half_tanh(0, early + late)
-            for u in range(UNITS + KEEP_LAG):
-                following = u + 1
-                if following < UNITS:
-                    if following % CHUNK_UNITS == 0 and following // CHUNK_UNITS + 1 < CHUNKS:
-                        load_weights(following // CHUNK_UNITS + 1)
-                    scores(following, early)
-                if 0 <= u - SUM_LAG < UNITS:
-                    window_sums(u - SUM_LAG)
-                if u < UNITS:
-                    shift_and_gate(u)
-                if 0 <= u - 1 < UNITS:
-                    weigh(u - 1)
-                if u >= KEEP_LAG:
-                    keep_sums(u - KEEP_LAG)
-                if following < UNITS:
-                    half_tanh(following, early)
-                if following < UNITS:
-                    scores(following, late)
-                    half_tanh(following, late)
-
-            for c in range(CHUNKS):
-                denominator = totals[:, 0, :, c * CHUNK : (c + 1) * CHUNK]
-                nc.scalar.activation(out=denominator, in_=denominator, func=ACT.Ln)
-            for c in range(CHUNKS):
-                denominator = totals[:, 0, :, c * CHUNK : (c + 1) * CHUNK]
-                numerator = totals[:, 1, :, c * CHUNK : (c + 1) * CHUNK]
-                nc.scalar.activation(out=denominator, in_=denominator, func=ACT.Exp, scale=-1.0)
+        def shift_and_gate(u):
+            def gate(j):
+                z = gated[u][:, 2 * j : 2 * j + 2, :]
                 nc.vector.scalar_tensor_tensor(
-                    out=numerator, in0=numerator, scalar=0.5, in1=denominator, op0=ALU.mult, op1=ALU.mult
+                    out=z, in0=z, scalar=1.0, in1=score_banks[u, j][:], op0=ALU.add, op1=ALU.mult
                 )
-                nc.sync.dma_start(out=out_dram[:, :, c * CHUNK : (c + 1) * CHUNK], in_=numerator)
+
+            lane_max = small.tile([P, 2, HALF], F32, name="lane_max")
+            nc.vector.tensor_tensor(out=lane_max[:], in0=score_banks[u, 1][:], in1=first_bank[u][:], op=ALU.max)
+            gate(0)
+            for j in range(2, BANKS):
+                nc.vector.tensor_tensor(out=lane_max[:], in0=score_banks[u, j][:], in1=lane_max[:], op=ALU.max)
+                gate(j - 1)
+            top[u] = small.tile([P, HALF], F32, name="top")
+            nc.vector.tensor_reduce(
+                out=top[u][:], in_=lane_max[:].rearrange("p l n -> p n l"), op=ALU.max, axis=AXIS.X
+            )
+            gate(BANKS - 1)
+            top_twice = top[u][:].unsqueeze(1).to_broadcast([P, 2, HALF])
+            shifted[u] = shifted_pool.tile([P, WINDOWS, HALF], F32, name="shifted")
+            nc.gpsimd.tensor_tensor(
+                out=shifted[u][:, 0:2, :], in0=first_bank[u][:], in1=top_twice, op=ALU.subtract
+            )
+            for j in range(1, BANKS):
+                nc.vector.tensor_tensor(
+                    out=shifted[u][:, 2 * j : 2 * j + 2, :],
+                    in0=score_banks[u, j][:],
+                    in1=top_twice,
+                    op=ALU.subtract,
+                )
+
+        def weigh(u):
+            nc.scalar.activation(out=shifted[u][:], in_=shifted[u][:], func=ACT.Exp)
+            engine = nc.gpsimd if u < UNITS - 2 else nc.vector
+            engine.tensor_tensor(out=gated[u][:], in0=shifted[u][:], in1=gated[u][:], op=ALU.mult)
+
+        def window_sum(u, which):
+            if which == 0:
+                both_sums[u] = sums.tile([P, 2, BLOCKS, P], F32, name="both_sums", tag="sum_bank")
+            terms = (shifted[u], gated[u])[which]
+            for b in range(BLOCKS):
+                for w in range(WINDOWS):
+                    nc.tensor.matmul(
+                        out=both_sums[u][:, which, b, :],
+                        lhsT=terms[:, w, b * P : (b + 1) * P],
+                        rhs=ident[:],
+                        is_transpose=True,
+                        start=(w == 0),
+                        stop=(w == WINDOWS - 1),
+                    )
+
+        def keep_sums(u):
+            c, half, t = place(u)
+            nc.scalar.copy(
+                out=totals[:, :, half * BLOCKS : (half + 1) * BLOCKS, t * P : (t + 1) * P],
+                in_=both_sums[u][:],
+            )
+
+        def piece(which, c, half):
+            return totals[:, which, half * BLOCKS : (half + 1) * BLOCKS, c * CHUNK : (c + 1) * CHUNK]
+
+        def logarithm(c, half):
+            nc.scalar.activation(out=piece(0, c, half), in_=piece(0, c, half), func=ACT.Ln)
+
+        def divide_and_store(c, half):
+            nc.scalar.activation(out=piece(0, c, half), in_=piece(0, c, half), func=ACT.Exp, scale=-1.0)
+            nc.vector.scalar_tensor_tensor(
+                out=piece(1, c, half),
+                in0=piece(1, c, half),
+                scalar=0.5,
+                in1=piece(0, c, half),
+                op0=ALU.mult,
+                op1=ALU.mult,
+            )
+            nc.sync.dma_start(
+                out=out_dram[:, half * BLOCKS : (half + 1) * BLOCKS, c * CHUNK : (c + 1) * CHUNK],
+                in_=piece(1, c, half),
+            )
+
+        load_rows(0, 0)
+        load_rows(0, 1)
+        load_planes()
+        load_weights(0, (0,))
+        load_rows(0, 2)
+        load_rows(0, 3)
+        load_weights(0, (1,))
+        for pair in range(PAIRS):
+            load_rows(1, pair)
+        load_weights(0, (2, 3))
+        load_weights(1, (0, 1, 2, 3))
+
+        early, late = (0, 1), (2, 3)
+        for pair in range(PAIRS):
+            if pair < PAIRS - 1:
+                flip(0, pair, banks, "bank")
+            else:
+                scores(0, (0,))
+                flip(0, pair, sums, "sum_bank")
+            regroup_block(0, pair, 0, nc.vector.tensor_copy)
+            regroup_block(0, pair, 1, nc.scalar.copy)
+            if pair > 0:
+                quantise(0, pair - 1)
+            if pair == PAIRS - 1:
+                half_tanh(0, (0,))
+        quantise(0, PAIRS - 1)
+        scores(0, (1, 2, 3))
+        half_tanh(0, (1, 2, 3))
+
+        for u in range(UNITS + NUMERATOR_LAG):
+            following = u + 1
+            if following < UNITS:
+                if following % CHUNK_UNITS == 0 and following // CHUNK_UNITS + 1 < CHUNKS:
+                    load_weights(following // CHUNK_UNITS + 1, (0, 1, 2, 3))
+                scores(following, early)
+            if 0 <= u - DENOMINATOR_LAG < UNITS:
+                window_sum(u - DENOMINATOR_LAG, 0)
+            if 0 <= u - NUMERATOR_LAG < UNITS:
+                window_sum(u - NUMERATOR_LAG, 1)
+            if u in (0, 1):
+                for pair in (2 * u, 2 * u + 1):
+                    flip(1, pair, sums, "sum_bank")
+                    for b in range(BLOCKS):
+                        regroup_block(1, pair, b, nc.scalar.copy)
+            if u in (1, 2):
+                for pair in (2 * u - 2, 2 * u - 1):
+                    quantise(1, pair)
+            if u < UNITS:
+                shift_and_gate(u)
+            if 0 <= u - 1 < UNITS:
+                weigh(u - 1)
+            if following < UNITS:
+                half_tanh(following, early)
+                scores(following, late)
+                half_tanh(following, late)
+            if 0 <= u - NUMERATOR_LAG < UNITS:
+                keep_sums(u - NUMERATOR_LAG)
+            if u == UNITS:
+                for c in range(CHUNKS):
+                    for half in range(HALVES):
+                        if (c, half) != (CHUNKS - 1, HALVES - 1):
+                            logarithm(c, half)
+
+        logarithm(CHUNKS - 1, HALVES - 1)
+        for c in range(CHUNKS):
+            for half in range(HALVES):
+                divide_and_store(c, half)

@@ -33,6 +33,7 @@ CHUNK_UNITS = CHUNK_TILES * HALVES
 
 DENOMINATOR_LAG = 2
 NUMERATOR_LAG = 3
+SQUARED_BY_SCALAR = 3
 
 
 def place(u):
@@ -228,11 +229,16 @@ def tile_dendriticlayersilu_ffn_kernel(tc, x, template_flat_words, template_flat
         def piece(which, c, half):
             return totals[:, which, half * BLOCKS : (half + 1) * BLOCKS, c * CHUNK : (c + 1) * CHUNK]
 
-        def logarithm(c, half):
-            nc.scalar.activation(out=piece(0, c, half), in_=piece(0, c, half), func=ACT.Ln)
+        def inverse_root(c, half):
+            nc.scalar.activation(out=piece(0, c, half), in_=piece(0, c, half), func=ACT.Abs_reciprocal_sqrt)
 
-        def divide_and_store(c, half):
-            nc.scalar.activation(out=piece(0, c, half), in_=piece(0, c, half), func=ACT.Exp, scale=-1.0)
+        def square(c, half):
+            nc.scalar.activation(out=piece(0, c, half), in_=piece(0, c, half), func=ACT.Square)
+
+        def times(c, half):
+            nc.vector.tensor_tensor(out=piece(1, c, half), in0=piece(1, c, half), in1=piece(0, c, half), op=ALU.mult)
+
+        def half_times_and_store(c, half):
             nc.vector.scalar_tensor_tensor(
                 out=piece(1, c, half),
                 in0=piece(1, c, half),
@@ -258,6 +264,7 @@ def tile_dendriticlayersilu_ffn_kernel(tc, x, template_flat_words, template_flat
         load_weights(0, (2, 3))
         load_weights(1, (0, 1, 2, 3))
 
+        pieces = [(c, half) for c in range(CHUNKS) for half in range(HALVES)]
         early, late = (0, 1), (2, 3)
         for pair in range(PAIRS):
             if pair < PAIRS - 1:
@@ -304,12 +311,17 @@ def tile_dendriticlayersilu_ffn_kernel(tc, x, template_flat_words, template_flat
             if 0 <= u - NUMERATOR_LAG < UNITS:
                 keep_sums(u - NUMERATOR_LAG)
             if u == UNITS:
-                for c in range(CHUNKS):
-                    for half in range(HALVES):
-                        if (c, half) != (CHUNKS - 1, HALVES - 1):
-                            logarithm(c, half)
+                for c, half in pieces[:-1]:
+                    inverse_root(c, half)
 
-        logarithm(CHUNKS - 1, HALVES - 1)
-        for c in range(CHUNKS):
-            for half in range(HALVES):
-                divide_and_store(c, half)
+        inverse_root(*pieces[-1])
+        for c, half in pieces[-SQUARED_BY_SCALAR:]:
+            square(c, half)
+        by_vector = pieces[:-SQUARED_BY_SCALAR]
+        for i in range(len(by_vector) + 1):
+            if i < len(by_vector):
+                times(*by_vector[i])
+            if i > 0:
+                half_times_and_store(*by_vector[i - 1])
+        for c, half in pieces[-SQUARED_BY_SCALAR:]:
+            half_times_and_store(c, half)

@@ -252,12 +252,10 @@ def tile_dendriticlayersilu_ffn_kernel(tc, x, template_flat_words, template_flat
                 in_=piece(1, c, half),
             )
 
-        load_rows(0, 0)
-        load_rows(0, 1)
+        for pair in range(PAIRS):
+            load_rows(0, pair)
         load_planes()
         load_weights(0, (0,))
-        load_rows(0, 2)
-        load_rows(0, 3)
         load_weights(0, (1,))
         for pair in range(PAIRS):
             load_rows(1, pair)
@@ -270,17 +268,14 @@ def tile_dendriticlayersilu_ffn_kernel(tc, x, template_flat_words, template_flat
             if pair < PAIRS - 1:
                 flip(0, pair, banks, "bank")
             else:
-                scores(0, (0,))
                 flip(0, pair, sums, "sum_bank")
             regroup_block(0, pair, 0, nc.vector.tensor_copy)
             regroup_block(0, pair, 1, nc.scalar.copy)
             if pair > 0:
                 quantise(0, pair - 1)
-            if pair == PAIRS - 1:
-                half_tanh(0, (0,))
         quantise(0, PAIRS - 1)
-        scores(0, (1, 2, 3))
-        half_tanh(0, (1, 2, 3))
+        scores(0, early + late)
+        half_tanh(0, early + late)
 
         for u in range(UNITS + NUMERATOR_LAG):
             following = u + 1

@@ -188,10 +188,11 @@ def tile_dendriticlayersilu_ffn_kernel(tc, x, template_flat_words, template_flat
             gate(BANKS - 1)
             top_twice = top[u][:].unsqueeze(1).to_broadcast([P, 2, HALF])
             shifted[u] = shifted_pool.tile([P, WINDOWS, HALF], F32, name="shifted")
-            nc.gpsimd.tensor_tensor(
-                out=shifted[u][:, 0:2, :], in0=first_bank[u][:], in1=top_twice, op=ALU.subtract
-            )
-            for j in range(1, BANKS):
+            if u < UNITS - 1:
+                nc.gpsimd.tensor_tensor(
+                    out=shifted[u][:, 0:2, :], in0=first_bank[u][:], in1=top_twice, op=ALU.subtract
+                )
+            for j in range(1 if u < UNITS - 1 else 0, BANKS):
                 nc.vector.tensor_tensor(
                     out=shifted[u][:, 2 * j : 2 * j + 2, :],
                     in0=score_banks[u, j][:],
@@ -200,13 +201,20 @@ def tile_dendriticlayersilu_ffn_kernel(tc, x, template_flat_words, template_flat
                 )
 
         def weigh(u):
-            nc.scalar.activation(out=shifted[u][:], in_=shifted[u][:], func=ACT.Exp)
+            if u < UNITS - 1:
+                nc.scalar.activation(out=shifted[u][:], in_=shifted[u][:], func=ACT.Exp)
+            else:
+                for j in range(BANKS):
+                    two = shifted[u][:, 2 * j : 2 * j + 2, :]
+                    nc.scalar.activation(out=two, in_=two, func=ACT.Exp)
             engine = nc.gpsimd if u < UNITS - 2 else nc.vector
             engine.tensor_tensor(out=gated[u][:], in0=shifted[u][:], in1=gated[u][:], op=ALU.mult)
 
         def window_sum(u, which):
-            if which == 0:
+            if which == 0 and u < UNITS - 2:
                 both_sums[u] = sums.tile([P, 2, BLOCKS, P], F32, name="both_sums", tag="sum_bank")
+            if which == 0 and u >= UNITS - 2:
+                both_sums[u] = banks.tile([P, 2, BLOCKS, P], F32, name="last_sums", tag="bank")
             terms = (shifted[u], gated[u])[which]
             for b in range(BLOCKS):
                 for w in range(WINDOWS):
@@ -303,11 +311,11 @@ def tile_dendriticlayersilu_ffn_kernel(tc, x, template_flat_words, template_flat
                 half_tanh(following, early)
                 scores(following, late)
                 half_tanh(following, late)
-            if 0 <= u - NUMERATOR_LAG < UNITS:
-                keep_sums(u - NUMERATOR_LAG)
             if u == UNITS:
                 for c, half in pieces[:-1]:
                     inverse_root(c, half)
+            if 0 <= u - NUMERATOR_LAG < UNITS:
+                keep_sums(u - NUMERATOR_LAG)
 
         inverse_root(*pieces[-1])
         for c, half in pieces[-SQUARED_BY_SCALAR:]:

@@ -86,12 +86,13 @@ def tile_dendriticlayersilu_ffn_kernel(tc, x, template_flat_words, template_flat
                 in_=words_dram[:, :, c * CHUNK + cols.start : c * CHUNK + cols.stop],
             )
 
-        def load_planes():
+        def load_planes(first_chunk, chunks):
+            cols = slice(first_chunk * CHUNK, (first_chunk + chunks) * CHUNK)
             for a in range(WINDOWS // 4):
                 for q in range(4):
                     nc.sync.dma_start(
-                        out=w_planes[32 * q : 32 * q + 16, a, :].bitcast(I32),
-                        in_=scales_dram[4 * a : 4 * a + 4, 4 * q : 4 * q + 4, :],
+                        out=w_planes[32 * q : 32 * q + 16, a, cols].bitcast(I32),
+                        in_=scales_dram[4 * a : 4 * a + 4, 4 * q : 4 * q + 4, cols.start // 4 : cols.stop // 4],
                     )
 
         x_rows = {}
@@ -262,12 +263,13 @@ def tile_dendriticlayersilu_ffn_kernel(tc, x, template_flat_words, template_flat
 
         for pair in range(PAIRS):
             load_rows(0, pair)
-        load_planes()
+        load_planes(0, 1)
         load_weights(0, (0,))
         load_weights(0, (1,))
         for pair in range(PAIRS):
             load_rows(1, pair)
         load_weights(0, (2, 3))
+        load_planes(1, CHUNKS - 1)
         load_weights(1, (0, 1, 2, 3))
 
         pieces = [(c, half) for c in range(CHUNKS) for half in range(HALVES)]

@@ -33,7 +33,8 @@ CHUNK_UNITS = CHUNK_TILES * HALVES
 
 DENOMINATOR_LAG = 2
 NUMERATOR_LAG = 3
-SQUARED_BY_SCALAR = 3
+PAIR = 2
+FIRST_LATE_PAIR = (UNITS - CHUNK_TILES) // PAIR
 
 
 def place(u):
@@ -139,7 +140,7 @@ def tile_dendriticlayersilu_ffn_kernel(tc, x, template_flat_words, template_flat
         top = {}
         shifted = {}
         gated = {}
-        both_sums = {}
+        sum_banks = {}
 
         def scores(u, which_banks):
             c, half, t = place(u)
@@ -212,15 +213,16 @@ def tile_dendriticlayersilu_ffn_kernel(tc, x, template_flat_words, template_flat
             engine.tensor_tensor(out=gated[u][:], in0=shifted[u][:], in1=gated[u][:], op=ALU.mult)
 
         def window_sum(u, which):
-            if which == 0 and u < UNITS - 2:
-                both_sums[u] = sums.tile([P, 2, BLOCKS, P], F32, name="both_sums", tag="sum_bank")
-            if which == 0 and u >= UNITS - 2:
-                both_sums[u] = banks.tile([P, 2, BLOCKS, P], F32, name="last_sums", tag="bank")
+            k, i = divmod(u, PAIR)
+            if i == 0 and u < UNITS - PAIR:
+                sum_banks[which, k] = sums.tile([P, BLOCKS, PAIR, P], F32, name="sum_bank", tag="sum_bank")
+            if i == 0 and u >= UNITS - PAIR:
+                sum_banks[which, k] = banks.tile([P, BLOCKS, PAIR, P], F32, name="last_sums", tag="bank")
             terms = (shifted[u], gated[u])[which]
             for b in range(BLOCKS):
                 for w in range(WINDOWS):
                     nc.tensor.matmul(
-                        out=both_sums[u][:, which, b, :],
+                        out=sum_banks[which, k][:, b, i, :],
                         lhsT=terms[:, w, b * P : (b + 1) * P],
                         rhs=ident[:],
                         is_transpose=True,
@@ -228,12 +230,21 @@ def tile_dendriticlayersilu_ffn_kernel(tc, x, template_flat_words, template_flat
                         stop=(w == WINDOWS - 1),
                     )
 
-        def keep_sums(u):
-            c, half, t = place(u)
-            nc.scalar.copy(
-                out=totals[:, :, half * BLOCKS : (half + 1) * BLOCKS, t * P : (t + 1) * P],
-                in_=both_sums[u][:],
-            )
+        def kept(which, k):
+            c, half, t = place(k * PAIR)
+            return totals[:, which, half * BLOCKS : (half + 1) * BLOCKS, t * P : (t + PAIR) * P]
+
+        def full_bank(which, k):
+            return sum_banks[which, k][:].rearrange("p b i f -> p b (i f)")
+
+        def keep_sums(u, which):
+            k, i = divmod(u, PAIR)
+            if i < PAIR - 1:
+                return
+            if which == 0:
+                nc.scalar.activation(out=kept(0, k), in_=full_bank(0, k), func=ACT.Square, scale=2.0)
+            elif k < FIRST_LATE_PAIR:
+                nc.scalar.copy(out=kept(1, k), in_=full_bank(1, k))
 
         def piece(which, c, half):
             return totals[:, which, half * BLOCKS : (half + 1) * BLOCKS, c * CHUNK : (c + 1) * CHUNK]
@@ -241,21 +252,15 @@ def tile_dendriticlayersilu_ffn_kernel(tc, x, template_flat_words, template_flat
         def inverse_root(c, half):
             nc.scalar.activation(out=piece(0, c, half), in_=piece(0, c, half), func=ACT.Abs_reciprocal_sqrt)
 
-        def square(c, half):
-            nc.scalar.activation(out=piece(0, c, half), in_=piece(0, c, half), func=ACT.Square)
-
-        def times(c, half):
-            nc.vector.tensor_tensor(out=piece(1, c, half), in0=piece(1, c, half), in1=piece(0, c, half), op=ALU.mult)
-
-        def half_times_and_store(c, half):
-            nc.vector.scalar_tensor_tensor(
-                out=piece(1, c, half),
-                in0=piece(1, c, half),
-                scalar=0.5,
-                in1=piece(0, c, half),
-                op0=ALU.mult,
-                op1=ALU.mult,
+        def finish_late_pair(k):
+            c, half, t = place(k * PAIR)
+            nc.vector.tensor_tensor(out=kept(1, k), in0=full_bank(1, k), in1=kept(0, k), op=ALU.mult)
+            nc.sync.dma_start(
+                out=out_dram[:, half * BLOCKS : (half + 1) * BLOCKS, t * P : (t + PAIR) * P], in_=kept(1, k)
             )
+
+        def divide_and_store(c, half):
+            nc.vector.tensor_tensor(out=piece(1, c, half), in0=piece(1, c, half), in1=piece(0, c, half), op=ALU.mult)
             nc.sync.dma_start(
                 out=out_dram[:, half * BLOCKS : (half + 1) * BLOCKS, c * CHUNK : (c + 1) * CHUNK],
                 in_=piece(1, c, half),
@@ -316,17 +321,16 @@ def tile_dendriticlayersilu_ffn_kernel(tc, x, template_flat_words, template_flat
             if u == UNITS:
                 for c, half in pieces[:-1]:
                     inverse_root(c, half)
+                for k in range(FIRST_LATE_PAIR, UNITS // PAIR - 1):
+                    nc.scalar.activation(out=kept(0, k), in_=kept(0, k), func=ACT.Abs_reciprocal_sqrt)
+            if 0 <= u - DENOMINATOR_LAG < UNITS:
+                keep_sums(u - DENOMINATOR_LAG, 0)
             if 0 <= u - NUMERATOR_LAG < UNITS:
-                keep_sums(u - NUMERATOR_LAG)
+                keep_sums(u - NUMERATOR_LAG, 1)
 
-        inverse_root(*pieces[-1])
-        for c, half in pieces[-SQUARED_BY_SCALAR:]:
-            square(c, half)
-        by_vector = pieces[:-SQUARED_BY_SCALAR]
-        for i in range(len(by_vector) + 1):
-            if i < len(by_vector):
-                times(*by_vector[i])
-            if i > 0:
-                half_times_and_store(*by_vector[i - 1])
-        for c, half in pieces[-SQUARED_BY_SCALAR:]:
-            half_times_and_store(c, half)
+        last_pair = UNITS // PAIR - 1
+        nc.scalar.activation(out=kept(0, last_pair), in_=kept(0, last_pair), func=ACT.Abs_reciprocal_sqrt)
+        for c, half in pieces[:-1]:
+            divide_and_store(c, half)
+        for k in range(FIRST_LATE_PAIR, UNITS // PAIR):
+            finish_late_pair(k)

@@ -177,17 +177,21 @@ def tile_dendriticlayersilu_ffn_kernel(tc, x, template_flat_words, template_flat
                     out=z, in0=z, scalar=1.0, in1=score_banks[u, j][:], op0=ALU.add, op1=ALU.mult
                 )
 
+            between = u < UNITS - 1
             lane_max = small.tile([P, 2, HALF], F32, name="lane_max")
             nc.vector.tensor_tensor(out=lane_max[:], in0=score_banks[u, 1][:], in1=first_bank[u][:], op=ALU.max)
-            gate(0)
+            if between:
+                gate(0)
             for j in range(2, BANKS):
                 nc.vector.tensor_tensor(out=lane_max[:], in0=score_banks[u, j][:], in1=lane_max[:], op=ALU.max)
-                gate(j - 1)
+                if between:
+                    gate(j - 1)
             top[u] = small.tile([P, HALF], F32, name="top")
             nc.vector.tensor_reduce(
                 out=top[u][:], in_=lane_max[:].rearrange("p l n -> p n l"), op=ALU.max, axis=AXIS.X
             )
-            gate(BANKS - 1)
+            if between:
+                gate(BANKS - 1)
             top_twice = top[u][:].unsqueeze(1).to_broadcast([P, 2, HALF])
             shifted[u] = shifted_pool.tile([P, WINDOWS, HALF], F32, name="shifted")
             if u < UNITS - 1:
@@ -201,6 +205,9 @@ def tile_dendriticlayersilu_ffn_kernel(tc, x, template_flat_words, template_flat
                     in1=top_twice,
                     op=ALU.subtract,
                 )
+            if not between:
+                for j in range(BANKS):
+                    gate(j)
 
         def weigh(u):
             if u < UNITS - 1:
@@ -209,7 +216,7 @@ def tile_dendriticlayersilu_ffn_kernel(tc, x, template_flat_words, template_flat
                 for j in range(BANKS):
                     two = shifted[u][:, 2 * j : 2 * j + 2, :]
                     nc.scalar.activation(out=two, in_=two, func=ACT.Exp)
-            engine = nc.gpsimd if u < UNITS - 2 else nc.vector
+            engine = nc.gpsimd if u < UNITS - 1 else nc.vector
             engine.tensor_tensor(out=gated[u][:], in0=shifted[u][:], in1=gated[u][:], op=ALU.mult)
 
         def window_sum(u, which):

import concourse.mybir as mybir
from concourse.masks import make_identity

F32 = mybir.dt.float32
BF16 = mybir.dt.bfloat16
I32 = mybir.dt.int32
U32 = mybir.dt.uint32
U8 = mybir.dt.uint8
FP8X4 = mybir.dt.float8_e4m3fn_x4
ACT = mybir.ActivationFunctionType
ALU = mybir.AluOpType
AXIS = mybir.AxisListType

P = 128
ROWS = 512
FEATURES = 2048
WINDOWS = 8
K_WINDOW = 512
FLOPS = 2 * ROWS * FEATURES * WINDOWS * K_WINDOW

ROW_TILES = ROWS // P
HALF = 256
BLOCKS = HALF // P
HALVES = ROWS // HALF
FEATURE_TILES = FEATURES // P
UNITS = FEATURE_TILES * HALVES
BANKS = 4
PAIRS = WINDOWS // 2
CHUNK_TILES = 4
CHUNK = CHUNK_TILES * P
CHUNKS = FEATURES // CHUNK
CHUNK_UNITS = CHUNK_TILES * HALVES

DENOMINATOR_LAG = 2
NUMERATOR_LAG = 3
PAIR = 2
FIRST_LATE_PAIR = (UNITS - CHUNK_TILES) // PAIR


def place(u):
    c, rest = divmod(u, CHUNK_UNITS)
    half, i = divmod(rest, CHUNK_TILES)
    return c, half, c * CHUNK_TILES + i


def tile_dendriticlayersilu_ffn_kernel(tc, x, template_flat_words, template_flat_scales, out):
    nc = tc.nc

    words_dram = (
        template_flat_words.rearrange("g p h t -> g p (h t)").bitcast(I32).rearrange("g p h -> p g h")
    )
    scales_dram = template_flat_scales.bitcast(I32)
    out_dram = out.rearrange("(b p) h -> p b h", p=P)

    with tc.manual_schedule(), tc.tile_pool(name="keep", bufs=1) as keep, tc.tile_pool(
        name="weights", bufs=2
    ) as weights, tc.tile_pool(name="rows", bufs=2 * PAIRS) as rows, tc.tile_pool(
        name="grouped", bufs=3
    ) as regroup, tc.tile_pool(name="shifted", bufs=4) as shifted_pool, tc.tile_pool(
        name="gated", bufs=5
    ) as gated_pool, tc.tile_pool(name="small", bufs=2) as small, tc.psum_pool(
        name="banks", bufs=6
    ) as banks, tc.psum_pool(name="sums", bufs=2) as sums:
        w_planes = keep.tile([P, WINDOWS // 4, FEATURES], U8, name="w_planes", align_bytes=64)
        nc.vector.memset(w_planes[:].rearrange("p a h -> p (a h)").bitcast(I32), 0)

        ident = keep.tile([P, P], F32, name="ident")
        make_identity(nc, ident[:])

        warm = keep.tile([P, 2], F32, name="warm")
        nc.vector.memset(warm[:], 0.0)
        nc.scalar.activation(out=warm[:, 1:2], in_=warm[:, 0:1], func=ACT.Tanh)

        x_codes = keep.tile([P, HALVES, WINDOWS, HALF], U32, name="x_codes", align_bytes=64)
        x_scales = keep.tile([P, HALVES, WINDOWS, HALF], U8, name="x_scales", align_bytes=64)

        totals = keep.tile([P, 2, ROW_TILES, FEATURES], F32, name="totals")

        w_chunks = {}

        def load_weights(c, tiles):
            if c not in w_chunks:
                w_chunks[c] = weights.tile([P, WINDOWS, CHUNK], U32, name="w_chunk", align_bytes=64)
            cols = slice(tiles[0] * P, (tiles[-1] + 1) * P)
            nc.sync.dma_start(
                out=w_chunks[c][:, :, cols].bitcast(I32),
                in_=words_dram[:, :, c * CHUNK + cols.start : c * CHUNK + cols.stop],
            )

        def load_planes(first_chunk, chunks):
            cols = slice(first_chunk * CHUNK, (first_chunk + chunks) * CHUNK)
            for a in range(WINDOWS // 4):
                for q in range(4):
                    nc.sync.dma_start(
                        out=w_planes[32 * q : 32 * q + 16, a, cols].bitcast(I32),
                        in_=scales_dram[4 * a : 4 * a + 4, 4 * q : 4 * q + 4, cols.start // 4 : cols.stop // 4],
                    )

        x_rows = {}
        flipped = {}
        grouped = {}

        def load_rows(half, pair):
            for b in range(BLOCKS):
                i = half * BLOCKS + b
                x_rows[half, pair, b] = rows.tile([P, 2 * K_WINDOW], BF16, name="x_rows")
                nc.sync.dma_start(
                    out=x_rows[half, pair, b][:],
                    in_=x[i * P : (i + 1) * P, 2 * pair * K_WINDOW : 2 * (pair + 1) * K_WINDOW],
                )

        def flip(half, pair, pool, tag):
            for b in range(BLOCKS):
                flipped[half, pair, b] = pool.tile([P, 2, 2, P], F32, name="flipped", tag=tag)
                x_words = x_rows[half, pair, b][:].bitcast(F32)
                for l in range(2):
                    for w in range(2):
                        nc.tensor.transpose(
                            flipped[half, pair, b][:, l, w, :], x_words[:, 256 * l + w : 256 * (l + 1) : 2], ident[:]
                        )

        def regroup_block(half, pair, b, copy):
            if b == 0:
                grouped[half, pair] = regroup.tile([P, 2, HALF, 4], BF16, name="grouped", align_bytes=64)
            copy(
                out=grouped[half, pair][:].bitcast(F32)[:, :, b * P : (b + 1) * P, :],
                in_=flipped[half, pair, b][:].rearrange("p l w n -> p l n w"),
            )

        def quantise(half, pair):
            two = slice(2 * pair, 2 * pair + 2)
            nc.vector.quantize_mx(
                out=x_codes[:, half, two, :].rearrange("p g n -> p (g n)").bitcast(FP8X4),
                scales=x_scales[:, half, two, :].rearrange("p g n -> p (g n)"),
                in_=grouped[half, pair][:].rearrange("p g n t -> p (g n t)"),
            )

        score_banks = {}
        first_bank = {}
        top = {}
        shifted = {}
        gated = {}
        sum_banks = {}

        def scores(u, which_banks):
            c, half, t = place(u)
            cols = slice((t % CHUNK_TILES) * P, (t % CHUNK_TILES + 1) * P)
            for j in which_banks:
                bank = banks.tile([P, 2, HALF], F32, name="score_bank", tag="bank")
                score_banks[u, j] = bank
                for l in range(2):
                    g = 2 * j + l
                    nc.tensor.matmul_mx(
                        out=bank[:, l, :],
                        lhsT=w_chunks[c][:, g, cols].bitcast(FP8X4),
                        lhsT_scale=w_planes[4 * (g % 4) : P, g // 4, t * P : (t + 1) * P],
                        rhs=x_codes[:, half, g, :].bitcast(FP8X4),
                        rhs_scale=x_scales[:, half, g, :],
                        start=True,
                        stop=True,
                    )

        def half_tanh(u, which_banks):
            for j in which_banks:
                if j == 0:
                    gated[u] = gated_pool.tile([P, WINDOWS, HALF], F32, name="gated")
                    first_bank[u] = small.tile([P, 2, HALF], F32, name="first_bank")
                    nc.scalar.copy(out=first_bank[u][:], in_=score_banks[u, 0][:])
                nc.scalar.activation(
                    out=gated[u][:, 2 * j : 2 * j + 2, :], in_=score_banks[u, j][:], func=ACT.Tanh, scale=0.5
                )

        def shift_and_gate(u):
            def gate(j):
                z = gated[u][:, 2 * j : 2 * j + 2, :]
                nc.vector.scalar_tensor_tensor(
                    out=z, in0=z, scalar=1.0, in1=score_banks[u, j][:], op0=ALU.add, op1=ALU.mult
                )

            between = u < UNITS - 1
            lane_max = small.tile([P, 2, HALF], F32, name="lane_max")
            nc.vector.tensor_tensor(out=lane_max[:], in0=score_banks[u, 1][:], in1=first_bank[u][:], op=ALU.max)
            if between:
                gate(0)
            for j in range(2, BANKS):
                nc.vector.tensor_tensor(out=lane_max[:], in0=score_banks[u, j][:], in1=lane_max[:], op=ALU.max)
                if between:
                    gate(j - 1)
            top[u] = small.tile([P, HALF], F32, name="top")
            nc.vector.tensor_reduce(
                out=top[u][:], in_=lane_max[:].rearrange("p l n -> p n l"), op=ALU.max, axis=AXIS.X
            )
            if between:
                gate(BANKS - 1)
            top_twice = top[u][:].unsqueeze(1).to_broadcast([P, 2, HALF])
            shifted[u] = shifted_pool.tile([P, WINDOWS, HALF], F32, name="shifted")
            if u < UNITS - 1:
                nc.gpsimd.tensor_tensor(
                    out=shifted[u][:, 0:2, :], in0=first_bank[u][:], in1=top_twice, op=ALU.subtract
                )
            for j in range(1 if u < UNITS - 1 else 0, BANKS):
                nc.vector.tensor_tensor(
                    out=shifted[u][:, 2 * j : 2 * j + 2, :],
                    in0=score_banks[u, j][:],
                    in1=top_twice,
                    op=ALU.subtract,
                )
            if not between:
                for j in range(BANKS):
                    gate(j)

        def weigh(u):
            if u < UNITS - 1:
                nc.scalar.activation(out=shifted[u][:], in_=shifted[u][:], func=ACT.Exp)
            else:
                for j in range(BANKS):
                    two = shifted[u][:, 2 * j : 2 * j + 2, :]
                    nc.scalar.activation(out=two, in_=two, func=ACT.Exp)
            engine = nc.gpsimd if u < UNITS - 1 else nc.vector
            engine.tensor_tensor(out=gated[u][:], in0=shifted[u][:], in1=gated[u][:], op=ALU.mult)

        def window_sum(u, which):
            k, i = divmod(u, PAIR)
            if i == 0 and u < UNITS - PAIR:
                sum_banks[which, k] = sums.tile([P, BLOCKS, PAIR, P], F32, name="sum_bank", tag="sum_bank")
            if i == 0 and u >= UNITS - PAIR:
                sum_banks[which, k] = banks.tile([P, BLOCKS, PAIR, P], F32, name="last_sums", tag="bank")
            terms = (shifted[u], gated[u])[which]
            for b in range(BLOCKS):
                for w in range(WINDOWS):
                    nc.tensor.matmul(
                        out=sum_banks[which, k][:, b, i, :],
                        lhsT=terms[:, w, b * P : (b + 1) * P],
                        rhs=ident[:],
                        is_transpose=True,
                        start=(w == 0),
                        stop=(w == WINDOWS - 1),
                    )

        def kept(which, k):
            c, half, t = place(k * PAIR)
            return totals[:, which, half * BLOCKS : (half + 1) * BLOCKS, t * P : (t + PAIR) * P]

        def full_bank(which, k):
            return sum_banks[which, k][:].rearrange("p b i f -> p b (i f)")

        def keep_sums(u, which):
            k, i = divmod(u, PAIR)
            if i < PAIR - 1:
                return
            if which == 0:
                nc.scalar.activation(out=kept(0, k), in_=full_bank(0, k), func=ACT.Square, scale=2.0)
            elif k < FIRST_LATE_PAIR:
                nc.scalar.copy(out=kept(1, k), in_=full_bank(1, k))

        def piece(which, c, half):
            return totals[:, which, half * BLOCKS : (half + 1) * BLOCKS, c * CHUNK : (c + 1) * CHUNK]

        def inverse_root(c, half):
            nc.scalar.activation(out=piece(0, c, half), in_=piece(0, c, half), func=ACT.Abs_reciprocal_sqrt)

        def finish_late_pair(k):
            c, half, t = place(k * PAIR)
            nc.vector.tensor_tensor(out=kept(1, k), in0=full_bank(1, k), in1=kept(0, k), op=ALU.mult)
            nc.sync.dma_start(
                out=out_dram[:, half * BLOCKS : (half + 1) * BLOCKS, t * P : (t + PAIR) * P], in_=kept(1, k)
            )

        def divide_and_store(c, half):
            nc.vector.tensor_tensor(out=piece(1, c, half), in0=piece(1, c, half), in1=piece(0, c, half), op=ALU.mult)
            nc.sync.dma_start(
                out=out_dram[:, half * BLOCKS : (half + 1) * BLOCKS, c * CHUNK : (c + 1) * CHUNK],
                in_=piece(1, c, half),
            )

        for pair in range(PAIRS):
            load_rows(0, pair)
        load_planes(0, 1)
        load_weights(0, (0,))
        load_weights(0, (1,))
        for pair in range(PAIRS):
            load_rows(1, pair)
        load_weights(0, (2, 3))
        load_planes(1, CHUNKS - 1)
        load_weights(1, (0, 1, 2, 3))

        pieces = [(c, half) for c in range(CHUNKS) for half in range(HALVES)]
        early, late = (0, 1), (2, 3)
        for pair in range(PAIRS):
            if pair < PAIRS - 1:
                flip(0, pair, banks, "bank")
            else:
                flip(0, pair, sums, "sum_bank")
            regroup_block(0, pair, 0, nc.vector.tensor_copy)
            regroup_block(0, pair, 1, nc.scalar.copy)
            if pair > 0:
                quantise(0, pair - 1)
        quantise(0, PAIRS - 1)
        scores(0, early + late)
        half_tanh(0, early + late)

        for u in range(UNITS + NUMERATOR_LAG):
            following = u + 1
            if following < UNITS:
                if following % CHUNK_UNITS == 0 and following // CHUNK_UNITS + 1 < CHUNKS:
                    load_weights(following // CHUNK_UNITS + 1, (0, 1, 2, 3))
                scores(following, early)
            if 0 <= u - DENOMINATOR_LAG < UNITS:
                window_sum(u - DENOMINATOR_LAG, 0)
            if 0 <= u - NUMERATOR_LAG < UNITS:
                window_sum(u - NUMERATOR_LAG, 1)
            if u in (0, 1):
                for pair in (2 * u, 2 * u + 1):
                    flip(1, pair, sums, "sum_bank")
                    for b in range(BLOCKS):
                        regroup_block(1, pair, b, nc.scalar.copy)
            if u in (1, 2):
                for pair in (2 * u - 2, 2 * u - 1):
                    quantise(1, pair)
            if u < UNITS:
                shift_and_gate(u)
            if 0 <= u - 1 < UNITS:
                weigh(u - 1)
            if following < UNITS:
                half_tanh(following, early)
                scores(following, late)
                half_tanh(following, late)
            if u == UNITS:
                for c, half in pieces[:-1]:
                    inverse_root(c, half)
                for k in range(FIRST_LATE_PAIR, UNITS // PAIR - 1):
                    nc.scalar.activation(out=kept(0, k), in_=kept(0, k), func=ACT.Abs_reciprocal_sqrt)
            if 0 <= u - DENOMINATOR_LAG < UNITS:
                keep_sums(u - DENOMINATOR_LAG, 0)
            if 0 <= u - NUMERATOR_LAG < UNITS:
                keep_sums(u - NUMERATOR_LAG, 1)

        last_pair = UNITS // PAIR - 1
        nc.scalar.activation(out=kept(0, last_pair), in_=kept(0, last_pair), func=ACT.Abs_reciprocal_sqrt)
        for c, half in pieces[:-1]:
            divide_and_store(c, half)
        for k in range(FIRST_LATE_PAIR, UNITS // PAIR):
            finish_late_pair(k)
